import numpy as np
import ml_dtypes


def mxq(x, axis, fmt="e4m3"):
    dtype, down = {"e4m3": (ml_dtypes.float8_e4m3fn, 7), "e5m2": (ml_dtypes.float8_e5m2, 14)}[fmt]
    v = np.moveaxis(np.asarray(x, np.float32).astype(ml_dtypes.bfloat16).astype(np.float64), axis, -1)
    blocks = v.reshape(v.shape[:-1] + (-1, 32))
    amax = np.abs(blocks).max(-1, keepdims=True)
    byte = np.maximum(np.where(amax > 0, np.frexp(amax)[1] - 1 + 127, 0) - down, 1)
    scale = np.exp2(byte - 127.0)
    codes = (blocks / scale).astype(np.float32).astype(dtype).astype(np.float64)
    return np.moveaxis((codes * scale).reshape(v.shape), -1, axis)


WIDE = False


def mx_kscale(k):
    if not WIDE:
        return np.ones(k)
    levels = np.array([10, -10, 5, -5, 0])
    a = np.random.permutation(np.resize(levels, k // 512 * 4)).reshape(k // 512, 4)
    idx = np.arange(k)
    return np.exp2(a[idx // 512, idx % 128 // 32])


BF16 = ml_dtypes.bfloat16


def bf(x):
    return np.asarray(x, np.float32).astype(BF16)


def f64(x):
    return np.asarray(x).astype(np.float64)


B, C, HH, WW, NH, HD, F = 32, 256, 16, 16, 8, 64, 1024
EPS = 1e-5


def layer_norm(v, w, b):
    mu = v.mean(-1, keepdims=True)
    var = ((v - mu) ** 2).mean(-1, keepdims=True)
    return (v - mu) * (1.0 / np.sqrt(var + EPS)) * w + b


def setup_inputs():
    s = mx_kscale(F)
    return {"h": bf(np.maximum(np.random.standard_normal((B, HH, WW, F)), 0.0) * 0.125 * s),
            "ffn2_w": bf(np.random.standard_normal((C, F)) * 0.5 / np.sqrt(F) / s),
            "ffn2_b": bf(np.random.standard_normal(C) * 0.02),
            "scale_ffn": bf(0.1 * (1.0 + 0.1 * np.random.standard_normal(1))),
            "ln2_w": bf(1.0 + 0.1 * np.random.standard_normal(C)),
            "ln2_b": bf(0.1 * np.random.standard_normal(C)),
            "scale_norm2": bf(1.5 * (1.0 + 0.1 * np.random.standard_normal(1))),
            "x": bf(np.random.standard_normal((B, C, HH, WW)))}


def reference(h, ffn2_w, ffn2_b, scale_ffn, ln2_w, ln2_b, scale_norm2, x):
    y2 = ((mxq(f64(h), 3, "e4m3") @ mxq(f64(ffn2_w), 1, "e4m3").T) + f64(ffn2_b)) * f64(scale_ffn)
    y2 = layer_norm(y2, f64(ln2_w), f64(ln2_b)) * f64(scale_norm2)
    out = np.maximum(y2 + f64(x).transpose(0, 2, 3, 1), 0.0)
    return out.transpose(0, 3, 1, 2)

@@ -1,0 +1,278 @@
+from contextlib import ExitStack
+
+import concourse.mybir as mybir
+from concourse.masks import make_identity
+
+F32 = mybir.dt.float32
+BF16 = mybir.dt.bfloat16
+U32 = mybir.dt.uint32
+U8 = mybir.dt.uint8
+FP8X4 = mybir.dt.float8_e4m3fn_x4
+ALU = mybir.AluOpType
+ACT = mybir.ActivationFunctionType
+
+P = 128
+K = 1024
+C = 256
+PIXELS = 32 * 16 * 16
+IMAGE = 16 * 16
+EPS = 1e-5
+PASSES = K // (4 * P)
+WORDS = K // 2
+BLOCKS = WORDS // P
+PARITIES = C // P
+TILES = 4
+GROUP = TILES * P
+GROUPS = PIXELS // GROUP
+IMAGES = GROUP // IMAGE
+
+PREFETCH = 3
+
+FLOPS = 2 * PIXELS * K * C
+
+
+def transpose_words(nc, bank, words, ident):
+    for j in range(BLOCKS):
+        nc.tensor.transpose(bank[:, j, :], words[:, j * P : (j + 1) * P], ident[:])
+
+
+def words_by_column(bank):
+    return bank[:].rearrange("p (g u) c -> p g c u", u=2)
+
+
+def tile_transformerconvblock_pc_t_kernel(
+    tc, h, ffn2_w, ffn2_b, scale_ffn, ln2_w, ln2_b, scale_norm2, x, out
+):
+    nc = tc.nc
+    h_rows = h.rearrange("b i j k -> (b i j) k")
+
+    with ExitStack() as ctx:
+        consts = ctx.enter_context(tc.tile_pool(name="consts", bufs=1))
+        h_pool = ctx.enter_context(tc.tile_pool(name="h_pool", bufs=5))
+        x_pool = ctx.enter_context(tc.tile_pool(name="x_pool", bufs=PREFETCH + 5))
+        mx_pool = ctx.enter_context(tc.tile_pool(name="mx_pool", bufs=2))
+        work = ctx.enter_context(tc.tile_pool(name="work", bufs=3))
+        stats = ctx.enter_context(tc.tile_pool(name="stats", bufs=4))
+        in_banks = ctx.enter_context(tc.psum_pool(name="in_banks", bufs=4))
+        acc_banks = ctx.enter_context(tc.psum_pool(name="acc_banks", bufs=2))
+        out_banks = ctx.enter_context(tc.psum_pool(name="out_banks", bufs=2))
+        ctx.enter_context(tc.manual_schedule())
+
+        ident = consts.tile([P, P], F32)
+        make_identity(nc, ident[:])
+        ones = consts.tile([P, P], BF16)
+        nc.vector.memset(ones[:], 1.0)
+        eps_col = consts.tile([P, 1], F32)
+        nc.vector.tensor_scalar(out=eps_col[:], in0=ones[:, 0:1], scalar1=EPS, scalar2=None, op0=ALU.mult)
+        warm = consts.tile([P, 1], F32)
+        nc.scalar.activation(out=warm[:], in_=eps_col[:], func=ACT.Sqrt)
+
+        S_AT = C
+        N_AT = C + 16
+        row = consts.tile([P, 512], BF16)
+        nc.vector.memset(row[:], 0.0)
+        nc.scalar.dma_start(out=row[0:1, 0:C], in_=ffn2_b.rearrange("(o c) -> o c", o=1))
+        nc.scalar.dma_start(out=row[0:1, S_AT : S_AT + 1], in_=scale_ffn.rearrange("(o c) -> o c", o=1))
+        nc.scalar.dma_start(out=row[0:1, N_AT : N_AT + 1], in_=scale_norm2.rearrange("(o c) -> o c", o=1))
+        ln_w = consts.tile([P, PARITIES], BF16)
+        nc.scalar.dma_start(out=ln_w[:], in_=ln2_w.rearrange("(q e) -> q e", e=PARITIES))
+        ln_b = consts.tile([P, PARITIES], BF16)
+        nc.scalar.dma_start(out=ln_b[:], in_=ln2_b.rearrange("(q e) -> q e", e=PARITIES))
+
+        w_sb = consts.tile([P, PARITIES * K], BF16)
+        nc.sync.dma_start(out=w_sb[:], in_=ffn2_w.rearrange("(q e) k -> q (e k)", e=PARITIES))
+
+        tiles = {}
+
+        def images_of(grp):
+            return slice(grp * IMAGES, (grp + 1) * IMAGES)
+
+        def load(grp):
+            h_sb = h_pool.tile([P, TILES * K], BF16, name="h_sb")
+            source = h_rows[grp * GROUP : (grp + 1) * GROUP, :].rearrange("(p t) k -> p (t k)", t=TILES)
+            pieces = TILES if grp == 0 else 1
+            width = TILES * K // pieces
+            for i in range(pieces):
+                cols = slice(i * width, (i + 1) * width)
+                nc.sync.dma_start(out=h_sb[:, cols], in_=source[:, cols])
+            x_sb = x_pool.tile([P, IMAGES, PARITIES, IMAGE], BF16, name="x_sb")
+            nc.sync.dma_start(
+                out=x_sb[:].rearrange("q b e s -> q b (e s)"),
+                in_=x[images_of(grp)].rearrange("b (q e) i j -> q b (e i j)", e=PARITIES),
+            )
+            tiles["h", grp] = h_sb
+            tiles["x", grp] = x_sb
+
+        for grp in range(PREFETCH):
+            load(grp)
+
+        w_words = w_sb[:].bitcast(F32)
+        w_grouped = consts.tile([P, PASSES * C * 4], BF16, align_bytes=64)
+        w_grouped_words = w_grouped[:].bitcast(F32).rearrange(
+            "p (g e q u) -> p g e q u", g=PASSES, e=PARITIES, u=2
+        )
+        for e in range(PARITIES):
+            w_bank = in_banks.tile([P, BLOCKS, P], F32, tag="in_bank")
+            transpose_words(nc, w_bank, w_words[:, e * WORDS : (e + 1) * WORDS], ident)
+            nc.vector.tensor_copy(out=w_grouped_words[:, :, e, :, :], in_=words_by_column(w_bank))
+        w_codes = consts.tile([P, PASSES * C], U32, align_bytes=64)
+        w_scales = consts.tile([P, PASSES * C], U8, align_bytes=64)
+        nc.vector.quantize_mx(out=w_codes[:].bitcast(FP8X4), scales=w_scales[:], in_=w_grouped[:])
+
+        row_bank = out_banks.tile([P, 512], F32, tag="out_bank")
+        nc.tensor.matmul(out=row_bank[:], lhsT=ones[:], rhs=row[:], start=True, stop=True)
+        bias_bc = consts.tile([P, C], F32)
+        nc.vector.tensor_copy(
+            out=bias_bc[:].rearrange("p (e q) -> p e q", e=PARITIES),
+            in_=row_bank[:, 0:C].rearrange("p (q e) -> p e q", e=PARITIES),
+        )
+        s_col = consts.tile([P, 1], F32)
+        nc.vector.tensor_copy(out=s_col[:], in_=row_bank[:, S_AT : S_AT + 1])
+        n_col = consts.tile([P, 1], F32)
+        nc.vector.tensor_copy(out=n_col[:], in_=row_bank[:, N_AT : N_AT + 1])
+        var_scale = consts.tile([P, 1], F32)
+        nc.vector.tensor_scalar(
+            out=var_scale[:], in0=s_col[:], scalar1=s_col[:, 0:1], scalar2=1.0 / C, op0=ALU.mult, op1=ALU.mult
+        )
+        gain = consts.tile([P, PARITIES], F32)
+        nc.vector.tensor_scalar(
+            out=gain[:], in0=ln_w[:], scalar1=n_col[:, 0:1], scalar2=s_col[:, 0:1], op0=ALU.mult, op1=ALU.mult
+        )
+        shift = consts.tile([P, PARITIES], F32)
+        nc.vector.tensor_scalar(out=shift[:], in0=ln_b[:], scalar1=n_col[:, 0:1], scalar2=None, op0=ALU.mult)
+
+        def transpose_in(grp):
+            h_words = tiles["h", grp][:].bitcast(F32)
+            h_grouped = mx_pool.tile([P, TILES * K], BF16, name="h_grouped", align_bytes=64)
+            h_grouped_words = h_grouped[:].bitcast(F32).rearrange(
+                "p (t g c u) -> p t g c u", t=TILES, g=PASSES, u=2
+            )
+            for t in range(TILES):
+                h_bank = in_banks.tile([P, BLOCKS, P], F32, tag="in_bank")
+                transpose_words(nc, h_bank, h_words[:, t * WORDS : (t + 1) * WORDS], ident)
+                nc.scalar.copy(out=h_grouped_words[:, t, :, :, :], in_=words_by_column(h_bank))
+            tiles["grouped", grp] = h_grouped
+
+        def quantise(grp):
+            h_codes = mx_pool.tile([P, TILES * PASSES * P], U32, name="h_codes", align_bytes=64)
+            h_scales = mx_pool.tile([P, TILES * PASSES * P], U8, name="h_scales", align_bytes=64)
+            nc.vector.quantize_mx(
+                out=h_codes[:].bitcast(FP8X4), scales=h_scales[:], in_=tiles["grouped", grp][:]
+            )
+            tiles["codes", grp] = h_codes
+            tiles["scales", grp] = h_scales
+
+        def multiply(grp):
+            h_codes = tiles["codes", grp]
+            h_scales = tiles["scales", grp]
+            v = work.tile([P, TILES, C], F32, name="v")
+            v_sum = stats.tile([P, TILES], F32, name="v_sum")
+            for first in range(0, TILES, 2):
+                acc = acc_banks.tile([P, 2, C], F32)
+                for t in (first, first + 1):
+                    for g in range(PASSES):
+                        px = slice((t * PASSES + g) * P, (t * PASSES + g + 1) * P)
+                        ch = slice(g * C, (g + 1) * C)
+                        nc.tensor.matmul_mx(
+                            out=acc[:, t - first, :],
+                            lhsT=h_codes[:, px].bitcast(FP8X4),
+                            lhsT_scale=h_scales[:, px],
+                            rhs=w_codes[:, ch].bitcast(FP8X4),
+                            rhs_scale=w_scales[:, ch],
+                            start=(g == 0),
+                            stop=(g == PASSES - 1),
+                        )
+                for t in (first, first + 1):
+                    nc.vector.scalar_tensor_tensor(
+                        out=v[:, t, :],
+                        in0=acc[:, t - first, :],
+                        scalar=1.0,
+                        in1=bias_bc[:],
+                        op0=ALU.mult,
+                        op1=ALU.add,
+                        accum_out=v_sum[:, t : t + 1],
+                    )
+            neg_mean = stats.tile([P, TILES], F32, name="neg_mean")
+            nc.vector.tensor_scalar(out=neg_mean[:], in0=v_sum[:], scalar1=-1.0 / C, scalar2=None, op0=ALU.mult)
+            tiles["v", grp] = v
+            tiles["neg_mean", grp] = neg_mean
+
+        def normalise(grp):
+            v = tiles["v", grp]
+            neg_mean = tiles["neg_mean", grp]
+            squares = work.tile([P, TILES, C], F32, name="squares")
+            sq_sum = stats.tile([P, TILES], F32, name="sq_sum")
+            for t in range(TILES):
+                nc.scalar.activation(
+                    out=squares[:, t, :],
+                    in_=v[:, t, :],
+                    func=ACT.Square,
+                    bias=neg_mean[:, t : t + 1],
+                    scale=1.0,
+                    accum_out=sq_sum[:, t : t + 1],
+                )
+            std = stats.tile([P, TILES], F32, name="std")
+            nc.scalar.activation(
+                out=std[:], in_=sq_sum[:], func=ACT.Sqrt, bias=eps_col[:, 0:1], scale=var_scale[:, 0:1]
+            )
+            rstd = stats.tile([P, TILES], F32, name="rstd")
+            nc.vector.reciprocal(out=rstd[:], in_=std[:])
+            normed = work.tile([P, TILES, C], F32, name="normed")
+            for t in range(TILES):
+                nc.vector.tensor_scalar(
+                    out=normed[:, t, :],
+                    in0=v[:, t, :],
+                    scalar1=neg_mean[:, t : t + 1],
+                    scalar2=rstd[:, t : t + 1],
+                    op0=ALU.add,
+                    op1=ALU.mult,
+                )
+            tiles["normed", grp] = normed
+
+        def transpose_out(grp):
+            normed = tiles["normed", grp]
+            x_sb = tiles["x", grp]
+            o_sb = work.tile([P, IMAGES, PARITIES, IMAGE], F32, name="o_sb")
+            for e in range(PARITIES):
+                o_bank = out_banks.tile([P, TILES, P], F32, tag="out_bank")
+                for t in range(TILES):
+                    nc.tensor.transpose(o_bank[:, t, :], normed[:, t, e * P : (e + 1) * P], ident[:])
+                nc.vector.scalar_tensor_tensor(
+                    out=o_sb[:, :, e, :].rearrange("q b (p t) -> q b p t", t=TILES),
+                    in0=o_bank[:].rearrange("q t (b p) -> q b p t", b=IMAGES),
+                    scalar=gain[:, e : e + 1],
+                    in1=x_sb[:, :, e, :].rearrange("q b (p t) -> q b p t", t=TILES),
+                    op0=ALU.mult,
+                    op1=ALU.add,
+                )
+            tiles["o", grp] = o_sb
+
+        def relu_store(grp):
+            o_sb = tiles["o", grp]
+            for e in range(PARITIES):
+                nc.scalar.activation(
+                    out=o_sb[:, :, e, :], in_=o_sb[:, :, e, :], func=ACT.Relu, bias=shift[:, e : e + 1], scale=1.0
+                )
+            nc.sync.dma_start(
+                out=out[images_of(grp)].rearrange("b (q e) i j -> q b (e i j)", e=PARITIES),
+                in_=o_sb[:].rearrange("q b e s -> q b (e s)"),
+            )
+
+        def is_group(grp):
+            return 0 <= grp < GROUPS
+
+        for step in range(GROUPS + 4):
+            if is_group(step + PREFETCH):
+                load(step + PREFETCH)
+            if is_group(step):
+                transpose_in(step)
+            if is_group(step - 1):
+                multiply(step - 1)
+            if is_group(step):
+                quantise(step)
+            if is_group(step - 2):
+                normalise(step - 2)
+            if is_group(step - 3):
+                transpose_out(step - 3)
+            if is_group(step - 4):
+                relu_store(step - 4)

@@ -49,10 +49,10 @@ def tile_transformerconvblock_pc_t_kernel(
     with ExitStack() as ctx:
         consts = ctx.enter_context(tc.tile_pool(name="consts", bufs=1))
         h_pool = ctx.enter_context(tc.tile_pool(name="h_pool", bufs=5))
-        x_pool = ctx.enter_context(tc.tile_pool(name="x_pool", bufs=PREFETCH + 5))
+        x_pool = ctx.enter_context(tc.tile_pool(name="x_pool", bufs=PREFETCH + 6))
         mx_pool = ctx.enter_context(tc.tile_pool(name="mx_pool", bufs=2))
         work = ctx.enter_context(tc.tile_pool(name="work", bufs=3))
-        stats = ctx.enter_context(tc.tile_pool(name="stats", bufs=4))
+        stats = ctx.enter_context(tc.tile_pool(name="stats", bufs=5))
         in_banks = ctx.enter_context(tc.psum_pool(name="in_banks", bufs=4))
         acc_banks = ctx.enter_context(tc.psum_pool(name="acc_banks", bufs=2))
         out_banks = ctx.enter_context(tc.psum_pool(name="out_banks", bufs=2))
@@ -62,10 +62,8 @@ def tile_transformerconvblock_pc_t_kernel(
         make_identity(nc, ident[:])
         ones = consts.tile([P, P], BF16)
         nc.vector.memset(ones[:], 1.0)
-        eps_col = consts.tile([P, 1], F32)
-        nc.vector.tensor_scalar(out=eps_col[:], in0=ones[:, 0:1], scalar1=EPS, scalar2=None, op0=ALU.mult)
-        warm = consts.tile([P, 1], F32)
-        nc.scalar.activation(out=warm[:], in_=eps_col[:], func=ACT.Sqrt)
+        minus_half = consts.tile([P, TILES], F32)
+        nc.vector.memset(minus_half[:], -0.5)
 
         S_AT = C
         N_AT = C + 16
@@ -165,7 +163,7 @@ def tile_transformerconvblock_pc_t_kernel(
         def multiply(grp):
             h_codes = tiles["codes", grp]
             h_scales = tiles["scales", grp]
-            v = work.tile([P, TILES, C], F32, name="v")
+            v = work.tile([P, TILES, C], F32, name="v", bufs=4)
             v_sum = stats.tile([P, TILES], F32, name="v_sum")
             for first in range(0, TILES, 2):
                 acc = acc_banks.tile([P, 2, C], F32)
@@ -192,34 +190,49 @@ def tile_transformerconvblock_pc_t_kernel(
                         op1=ALU.add,
                         accum_out=v_sum[:, t : t + 1],
                     )
-            neg_mean = stats.tile([P, TILES], F32, name="neg_mean")
-            nc.vector.tensor_scalar(out=neg_mean[:], in0=v_sum[:], scalar1=-1.0 / C, scalar2=None, op0=ALU.mult)
             tiles["v", grp] = v
+            tiles["v_sum", grp] = v_sum
+
+        def mean(grp):
+            neg_mean = stats.tile([P, TILES], F32, name="neg_mean")
+            nc.gpsimd.tensor_scalar(
+                out=neg_mean[:], in0=tiles["v_sum", grp][:], scalar1=-1.0 / C, scalar2=0.0, op0=ALU.mult, op1=ALU.add
+            )
             tiles["neg_mean", grp] = neg_mean
 
-        def normalise(grp):
+        def squares(grp):
             v = tiles["v", grp]
             neg_mean = tiles["neg_mean", grp]
-            squares = work.tile([P, TILES, C], F32, name="squares")
+            squared = work.tile([P, TILES, C], F32, name="squared", bufs=2)
             sq_sum = stats.tile([P, TILES], F32, name="sq_sum")
             for t in range(TILES):
                 nc.scalar.activation(
-                    out=squares[:, t, :],
+                    out=squared[:, t, :],
                     in_=v[:, t, :],
                     func=ACT.Square,
                     bias=neg_mean[:, t : t + 1],
                     scale=1.0,
                     accum_out=sq_sum[:, t : t + 1],
                 )
-            std = stats.tile([P, TILES], F32, name="std")
-            nc.scalar.activation(
-                out=std[:], in_=sq_sum[:], func=ACT.Sqrt, bias=eps_col[:, 0:1], scale=var_scale[:, 0:1]
+            tiles["sq_sum", grp] = sq_sum
+
+        def normalise(grp):
+            v = tiles["v", grp]
+            neg_mean = tiles["neg_mean", grp]
+            var_eps = stats.tile([P, TILES], F32, name="var_eps")
+            nc.gpsimd.tensor_scalar(
+                out=var_eps[:],
+                in0=tiles["sq_sum", grp][:],
+                scalar1=var_scale[:, 0:1],
+                scalar2=EPS,
+                op0=ALU.mult,
+                op1=ALU.add,
             )
             rstd = stats.tile([P, TILES], F32, name="rstd")
-            nc.vector.reciprocal(out=rstd[:], in_=std[:])
+            nc.gpsimd.tensor_tensor(out=rstd[:], in0=var_eps[:], in1=minus_half[:], op=ALU.pow)
             normed = work.tile([P, TILES, C], F32, name="normed")
             for t in range(TILES):
-                nc.vector.tensor_scalar(
+                nc.gpsimd.tensor_scalar(
                     out=normed[:, t, :],
                     in0=v[:, t, :],
                     scalar1=neg_mean[:, t : t + 1],
@@ -245,13 +258,14 @@ def tile_transformerconvblock_pc_t_kernel(
                     op0=ALU.mult,
                     op1=ALU.add,
                 )
-            tiles["o", grp] = o_sb
-
-        def relu_store(grp):
-            o_sb = tiles["o", grp]
             for e in range(PARITIES):
-                nc.scalar.activation(
-                    out=o_sb[:, :, e, :], in_=o_sb[:, :, e, :], func=ACT.Relu, bias=shift[:, e : e + 1], scale=1.0
+                nc.vector.tensor_scalar(
+                    out=o_sb[:, :, e, :],
+                    in0=o_sb[:, :, e, :],
+                    scalar1=shift[:, e : e + 1],
+                    scalar2=0.0,
+                    op0=ALU.add,
+                    op1=ALU.max,
                 )
             nc.sync.dma_start(
                 out=out[images_of(grp)].rearrange("b (q e) i j -> q b (e i j)", e=PARITIES),
@@ -271,8 +285,10 @@ def tile_transformerconvblock_pc_t_kernel(
             if is_group(step):
                 quantise(step)
             if is_group(step - 2):
-                normalise(step - 2)
+                squares(step - 2)
             if is_group(step - 3):
-                transpose_out(step - 3)
+                normalise(step - 3)
+            if is_group(step - 1):
+                mean(step - 1)
             if is_group(step - 4):
-                relu_store(step - 4)
+                transpose_out(step - 4)

@@ -22,6 +22,7 @@ WORDS = K // 2
 BLOCKS = WORDS // P
 PARITIES = C // P
 TILES = 4
+PAIR = 2
 GROUP = TILES * P
 GROUPS = PIXELS // GROUP
 IMAGES = GROUP // IMAGE
@@ -49,10 +50,10 @@ def tile_transformerconvblock_pc_t_kernel(
     with ExitStack() as ctx:
         consts = ctx.enter_context(tc.tile_pool(name="consts", bufs=1))
         h_pool = ctx.enter_context(tc.tile_pool(name="h_pool", bufs=5))
-        x_pool = ctx.enter_context(tc.tile_pool(name="x_pool", bufs=PREFETCH + 6))
+        x_pool = ctx.enter_context(tc.tile_pool(name="x_pool", bufs=PREFETCH + 5))
         mx_pool = ctx.enter_context(tc.tile_pool(name="mx_pool", bufs=2))
         work = ctx.enter_context(tc.tile_pool(name="work", bufs=3))
-        stats = ctx.enter_context(tc.tile_pool(name="stats", bufs=5))
+        stats = ctx.enter_context(tc.tile_pool(name="stats", bufs=4))
         in_banks = ctx.enter_context(tc.psum_pool(name="in_banks", bufs=4))
         acc_banks = ctx.enter_context(tc.psum_pool(name="acc_banks", bufs=2))
         out_banks = ctx.enter_context(tc.psum_pool(name="out_banks", bufs=2))
@@ -62,8 +63,10 @@ def tile_transformerconvblock_pc_t_kernel(
         make_identity(nc, ident[:])
         ones = consts.tile([P, P], BF16)
         nc.vector.memset(ones[:], 1.0)
-        minus_half = consts.tile([P, TILES], F32)
-        nc.vector.memset(minus_half[:], -0.5)
+        eps_col = consts.tile([P, 1], F32)
+        nc.vector.tensor_scalar(out=eps_col[:], in0=ones[:, 0:1], scalar1=EPS, scalar2=None, op0=ALU.mult)
+        warm = consts.tile([P, 1], F32)
+        nc.scalar.activation(out=warm[:], in_=eps_col[:], func=ACT.Sqrt)
 
         S_AT = C
         N_AT = C + 16
@@ -139,71 +142,73 @@ def tile_transformerconvblock_pc_t_kernel(
         shift = consts.tile([P, PARITIES], F32)
         nc.vector.tensor_scalar(out=shift[:], in0=ln_b[:], scalar1=n_col[:, 0:1], scalar2=None, op0=ALU.mult)
 
-        def transpose_in(grp):
+        def transpose_in(grp, half):
+            if half == 0:
+                tiles["grouped", grp] = mx_pool.tile([P, TILES * K], BF16, name="h_grouped", align_bytes=64)
             h_words = tiles["h", grp][:].bitcast(F32)
-            h_grouped = mx_pool.tile([P, TILES * K], BF16, name="h_grouped", align_bytes=64)
-            h_grouped_words = h_grouped[:].bitcast(F32).rearrange(
+            h_grouped_words = tiles["grouped", grp][:].bitcast(F32).rearrange(
                 "p (t g c u) -> p t g c u", t=TILES, g=PASSES, u=2
             )
-            for t in range(TILES):
+            for t in range(half * PAIR, (half + 1) * PAIR):
                 h_bank = in_banks.tile([P, BLOCKS, P], F32, tag="in_bank")
                 transpose_words(nc, h_bank, h_words[:, t * WORDS : (t + 1) * WORDS], ident)
                 nc.scalar.copy(out=h_grouped_words[:, t, :, :, :], in_=words_by_column(h_bank))
-            tiles["grouped", grp] = h_grouped
 
-        def quantise(grp):
-            h_codes = mx_pool.tile([P, TILES * PASSES * P], U32, name="h_codes", align_bytes=64)
-            h_scales = mx_pool.tile([P, TILES * PASSES * P], U8, name="h_scales", align_bytes=64)
+        def quantise(grp, half):
+            if half == 0:
+                tiles["codes", grp] = mx_pool.tile([P, TILES * PASSES * P], U32, name="h_codes", align_bytes=64)
+                tiles["scales", grp] = mx_pool.tile([P, TILES * PASSES * P], U8, name="h_scales", align_bytes=64)
+            words = slice(half * PAIR * PASSES * P, (half + 1) * PAIR * PASSES * P)
+            values = slice(half * PAIR * K, (half + 1) * PAIR * K)
             nc.vector.quantize_mx(
-                out=h_codes[:].bitcast(FP8X4), scales=h_scales[:], in_=tiles["grouped", grp][:]
+                out=tiles["codes", grp][:, words].bitcast(FP8X4),
+                scales=tiles["scales", grp][:, words],
+                in_=tiles["grouped", grp][:, values],
             )
-            tiles["codes", grp] = h_codes
-            tiles["scales", grp] = h_scales
 
-        def multiply(grp):
+        def multiply(grp, half):
+            if half == 0:
+                tiles["v", grp] = work.tile([P, TILES, C], F32, name="v")
+                tiles["v_sum", grp] = stats.tile([P, TILES], F32, name="v_sum")
             h_codes = tiles["codes", grp]
             h_scales = tiles["scales", grp]
-            v = work.tile([P, TILES, C], F32, name="v", bufs=4)
-            v_sum = stats.tile([P, TILES], F32, name="v_sum")
-            for first in range(0, TILES, 2):
-                acc = acc_banks.tile([P, 2, C], F32)
-                for t in (first, first + 1):
-                    for g in range(PASSES):
-                        px = slice((t * PASSES + g) * P, (t * PASSES + g + 1) * P)
-                        ch = slice(g * C, (g + 1) * C)
-                        nc.tensor.matmul_mx(
-                            out=acc[:, t - first, :],
-                            lhsT=h_codes[:, px].bitcast(FP8X4),
-                            lhsT_scale=h_scales[:, px],
-                            rhs=w_codes[:, ch].bitcast(FP8X4),
-                            rhs_scale=w_scales[:, ch],
-                            start=(g == 0),
-                            stop=(g == PASSES - 1),
-                        )
-                for t in (first, first + 1):
-                    nc.vector.scalar_tensor_tensor(
-                        out=v[:, t, :],
-                        in0=acc[:, t - first, :],
-                        scalar=1.0,
-                        in1=bias_bc[:],
-                        op0=ALU.mult,
-                        op1=ALU.add,
-                        accum_out=v_sum[:, t : t + 1],
+            acc = acc_banks.tile([P, PAIR, C], F32)
+            for i in range(PAIR):
+                for g in range(PASSES):
+                    px = slice(((half * PAIR + i) * PASSES + g) * P, ((half * PAIR + i) * PASSES + g + 1) * P)
+                    ch = slice(g * C, (g + 1) * C)
+                    nc.tensor.matmul_mx(
+                        out=acc[:, i, :],
+                        lhsT=h_codes[:, px].bitcast(FP8X4),
+                        lhsT_scale=h_scales[:, px],
+                        rhs=w_codes[:, ch].bitcast(FP8X4),
+                        rhs_scale=w_scales[:, ch],
+                        start=(g == 0),
+                        stop=(g == PASSES - 1),
                     )
-            tiles["v", grp] = v
-            tiles["v_sum", grp] = v_sum
+            for i in range(PAIR):
+                t = half * PAIR + i
+                nc.vector.scalar_tensor_tensor(
+                    out=tiles["v", grp][:, t, :],
+                    in0=acc[:, i, :],
+                    scalar=1.0,
+                    in1=bias_bc[:],
+                    op0=ALU.mult,
+                    op1=ALU.add,
+                    accum_out=tiles["v_sum", grp][:, t : t + 1],
+                )
 
         def mean(grp):
             neg_mean = stats.tile([P, TILES], F32, name="neg_mean")
-            nc.gpsimd.tensor_scalar(
-                out=neg_mean[:], in0=tiles["v_sum", grp][:], scalar1=-1.0 / C, scalar2=0.0, op0=ALU.mult, op1=ALU.add
+            nc.vector.tensor_scalar(
+                out=neg_mean[:], in0=tiles["v_sum", grp][:], scalar1=-1.0 / C, scalar2=None, op0=ALU.mult
             )
             tiles["neg_mean", grp] = neg_mean
 
         def squares(grp):
             v = tiles["v", grp]
             neg_mean = tiles["neg_mean", grp]
-            squared = work.tile([P, TILES, C], F32, name="squared", bufs=2)
+            squared = work.tile([P, TILES, C], F32, name="squared")
             sq_sum = stats.tile([P, TILES], F32, name="sq_sum")
             for t in range(TILES):
                 nc.scalar.activation(
@@ -214,25 +219,20 @@ def tile_transformerconvblock_pc_t_kernel(
                     scale=1.0,
                     accum_out=sq_sum[:, t : t + 1],
                 )
-            tiles["sq_sum", grp] = sq_sum
+            std = stats.tile([P, TILES], F32, name="std")
+            nc.scalar.activation(
+                out=std[:], in_=sq_sum[:], func=ACT.Sqrt, bias=eps_col[:, 0:1], scale=var_scale[:, 0:1]
+            )
+            tiles["std", grp] = std
 
         def normalise(grp):
             v = tiles["v", grp]
             neg_mean = tiles["neg_mean", grp]
-            var_eps = stats.tile([P, TILES], F32, name="var_eps")
-            nc.gpsimd.tensor_scalar(
-                out=var_eps[:],
-                in0=tiles["sq_sum", grp][:],
-                scalar1=var_scale[:, 0:1],
-                scalar2=EPS,
-                op0=ALU.mult,
-                op1=ALU.add,
-            )
             rstd = stats.tile([P, TILES], F32, name="rstd")
-            nc.gpsimd.tensor_tensor(out=rstd[:], in0=var_eps[:], in1=minus_half[:], op=ALU.pow)
+            nc.vector.reciprocal(out=rstd[:], in_=tiles["std", grp][:])
             normed = work.tile([P, TILES, C], F32, name="normed")
             for t in range(TILES):
-                nc.gpsimd.tensor_scalar(
+                nc.vector.tensor_scalar(
                     out=normed[:, t, :],
                     in0=v[:, t, :],
                     scalar1=neg_mean[:, t : t + 1],
@@ -242,30 +242,26 @@ def tile_transformerconvblock_pc_t_kernel(
                 )
             tiles["normed", grp] = normed
 
-        def transpose_out(grp):
-            normed = tiles["normed", grp]
-            x_sb = tiles["x", grp]
-            o_sb = work.tile([P, IMAGES, PARITIES, IMAGE], F32, name="o_sb")
+        def transpose_out(grp, e):
+            if e == 0:
+                tiles["o", grp] = work.tile([P, IMAGES, PARITIES, IMAGE], F32, name="o_sb")
+            o_bank = out_banks.tile([P, TILES, P], F32, tag="out_bank")
+            for t in range(TILES):
+                nc.tensor.transpose(o_bank[:, t, :], tiles["normed", grp][:, t, e * P : (e + 1) * P], ident[:])
+            nc.vector.scalar_tensor_tensor(
+                out=tiles["o", grp][:, :, e, :].rearrange("q b (p t) -> q b p t", t=TILES),
+                in0=o_bank[:].rearrange("q t (b p) -> q b p t", b=IMAGES),
+                scalar=gain[:, e : e + 1],
+                in1=tiles["x", grp][:, :, e, :].rearrange("q b (p t) -> q b p t", t=TILES),
+                op0=ALU.mult,
+                op1=ALU.add,
+            )
+
+        def relu_store(grp):
+            o_sb = tiles["o", grp]
             for e in range(PARITIES):
-                o_bank = out_banks.tile([P, TILES, P], F32, tag="out_bank")
-                for t in range(TILES):
-                    nc.tensor.transpose(o_bank[:, t, :], normed[:, t, e * P : (e + 1) * P], ident[:])
-                nc.vector.scalar_tensor_tensor(
-                    out=o_sb[:, :, e, :].rearrange("q b (p t) -> q b p t", t=TILES),
-                    in0=o_bank[:].rearrange("q t (b p) -> q b p t", b=IMAGES),
-                    scalar=gain[:, e : e + 1],
-                    in1=x_sb[:, :, e, :].rearrange("q b (p t) -> q b p t", t=TILES),
-                    op0=ALU.mult,
-                    op1=ALU.add,
-                )
-            for e in range(PARITIES):
-                nc.vector.tensor_scalar(
-                    out=o_sb[:, :, e, :],
-                    in0=o_sb[:, :, e, :],
-                    scalar1=shift[:, e : e + 1],
-                    scalar2=0.0,
-                    op0=ALU.add,
-                    op1=ALU.max,
+                nc.scalar.activation(
+                    out=o_sb[:, :, e, :], in_=o_sb[:, :, e, :], func=ACT.Relu, bias=shift[:, e : e + 1], scale=1.0
                 )
             nc.sync.dma_start(
                 out=out[images_of(grp)].rearrange("b (q e) i j -> q b (e i j)", e=PARITIES),
@@ -278,17 +274,28 @@ def tile_transformerconvblock_pc_t_kernel(
         for step in range(GROUPS + 4):
             if is_group(step + PREFETCH):
                 load(step + PREFETCH)
+
             if is_group(step):
-                transpose_in(step)
+                transpose_in(step, 0)
             if is_group(step - 1):
-                multiply(step - 1)
+                multiply(step - 1, 0)
+            if is_group(step - 4):
+                transpose_out(step - 4, 1)
             if is_group(step):
-                quantise(step)
+                quantise(step, 0)
             if is_group(step - 2):
                 squares(step - 2)
-            if is_group(step - 3):
-                normalise(step - 3)
+
+            if is_group(step):
+                transpose_in(step, 1)
             if is_group(step - 1):
+                multiply(step - 1, 1)
                 mean(step - 1)
+            if is_group(step - 3):
+                transpose_out(step - 3, 0)
+            if is_group(step - 2):
+                normalise(step - 2)
+            if is_group(step):
+                quantise(step, 1)
             if is_group(step - 4):
-                transpose_out(step - 4)
+                relu_store(step - 4)

from contextlib import ExitStack

import concourse.mybir as mybir
from concourse.masks import make_identity

F32 = mybir.dt.float32
BF16 = mybir.dt.bfloat16
U32 = mybir.dt.uint32
U8 = mybir.dt.uint8
FP8X4 = mybir.dt.float8_e4m3fn_x4
ALU = mybir.AluOpType
ACT = mybir.ActivationFunctionType

P = 128
K = 1024
C = 256
PIXELS = 32 * 16 * 16
IMAGE = 16 * 16
EPS = 1e-5
PASSES = K // (4 * P)
WORDS = K // 2
BLOCKS = WORDS // P
PARITIES = C // P
TILES = 4
PAIR = 2
GROUP = TILES * P
GROUPS = PIXELS // GROUP
IMAGES = GROUP // IMAGE

PREFETCH = 3

FLOPS = 2 * PIXELS * K * C


def transpose_words(nc, bank, words, ident):
    for j in range(BLOCKS):
        nc.tensor.transpose(bank[:, j, :], words[:, j * P : (j + 1) * P], ident[:])


def words_by_column(bank):
    return bank[:].rearrange("p (g u) c -> p g c u", u=2)


def tile_transformerconvblock_pc_t_kernel(
    tc, h, ffn2_w, ffn2_b, scale_ffn, ln2_w, ln2_b, scale_norm2, x, out
):
    nc = tc.nc
    h_rows = h.rearrange("b i j k -> (b i j) k")

    with ExitStack() as ctx:
        consts = ctx.enter_context(tc.tile_pool(name="consts", bufs=1))
        h_pool = ctx.enter_context(tc.tile_pool(name="h_pool", bufs=5))
        x_pool = ctx.enter_context(tc.tile_pool(name="x_pool", bufs=PREFETCH + 5))
        mx_pool = ctx.enter_context(tc.tile_pool(name="mx_pool", bufs=2))
        work = ctx.enter_context(tc.tile_pool(name="work", bufs=3))
        stats = ctx.enter_context(tc.tile_pool(name="stats", bufs=4))
        in_banks = ctx.enter_context(tc.psum_pool(name="in_banks", bufs=4))
        acc_banks = ctx.enter_context(tc.psum_pool(name="acc_banks", bufs=2))
        out_banks = ctx.enter_context(tc.psum_pool(name="out_banks", bufs=2))
        ctx.enter_context(tc.manual_schedule())

        ident = consts.tile([P, P], F32)
        make_identity(nc, ident[:])
        ones = consts.tile([P, P], BF16)
        nc.vector.memset(ones[:], 1.0)
        eps_col = consts.tile([P, 1], F32)
        nc.vector.tensor_scalar(out=eps_col[:], in0=ones[:, 0:1], scalar1=EPS, scalar2=None, op0=ALU.mult)
        warm = consts.tile([P, 1], F32)
        nc.scalar.activation(out=warm[:], in_=eps_col[:], func=ACT.Sqrt)

        S_AT = C
        N_AT = C + 16
        row = consts.tile([P, 512], BF16)
        nc.vector.memset(row[:], 0.0)
        nc.scalar.dma_start(out=row[0:1, 0:C], in_=ffn2_b.rearrange("(o c) -> o c", o=1))
        nc.scalar.dma_start(out=row[0:1, S_AT : S_AT + 1], in_=scale_ffn.rearrange("(o c) -> o c", o=1))
        nc.scalar.dma_start(out=row[0:1, N_AT : N_AT + 1], in_=scale_norm2.rearrange("(o c) -> o c", o=1))
        ln_w = consts.tile([P, PARITIES], BF16)
        nc.scalar.dma_start(out=ln_w[:], in_=ln2_w.rearrange("(q e) -> q e", e=PARITIES))
        ln_b = consts.tile([P, PARITIES], BF16)
        nc.scalar.dma_start(out=ln_b[:], in_=ln2_b.rearrange("(q e) -> q e", e=PARITIES))

        w_sb = consts.tile([P, PARITIES * K], BF16)
        nc.sync.dma_start(out=w_sb[:], in_=ffn2_w.rearrange("(q e) k -> q (e k)", e=PARITIES))

        tiles = {}

        def images_of(grp):
            return slice(grp * IMAGES, (grp + 1) * IMAGES)

        def load(grp):
            h_sb = h_pool.tile([P, TILES * K], BF16, name="h_sb")
            source = h_rows[grp * GROUP : (grp + 1) * GROUP, :].rearrange("(p t) k -> p (t k)", t=TILES)
            pieces = TILES if grp == 0 else 1
            width = TILES * K // pieces
            for i in range(pieces):
                cols = slice(i * width, (i + 1) * width)
                nc.sync.dma_start(out=h_sb[:, cols], in_=source[:, cols])
            x_sb = x_pool.tile([P, IMAGES, PARITIES, IMAGE], BF16, name="x_sb")
            nc.sync.dma_start(
                out=x_sb[:].rearrange("q b e s -> q b (e s)"),
                in_=x[images_of(grp)].rearrange("b (q e) i j -> q b (e i j)", e=PARITIES),
            )
            tiles["h", grp] = h_sb
            tiles["x", grp] = x_sb

        for grp in range(PREFETCH):
            load(grp)

        w_words = w_sb[:].bitcast(F32)
        w_grouped = consts.tile([P, PASSES * C * 4], BF16, align_bytes=64)
        w_grouped_words = w_grouped[:].bitcast(F32).rearrange(
            "p (g e q u) -> p g e q u", g=PASSES, e=PARITIES, u=2
        )
        for e in range(PARITIES):
            w_bank = in_banks.tile([P, BLOCKS, P], F32, tag="in_bank")
            transpose_words(nc, w_bank, w_words[:, e * WORDS : (e + 1) * WORDS], ident)
            nc.vector.tensor_copy(out=w_grouped_words[:, :, e, :, :], in_=words_by_column(w_bank))
        w_codes = consts.tile([P, PASSES * C], U32, align_bytes=64)
        w_scales = consts.tile([P, PASSES * C], U8, align_bytes=64)
        nc.vector.quantize_mx(out=w_codes[:].bitcast(FP8X4), scales=w_scales[:], in_=w_grouped[:])

        row_bank = out_banks.tile([P, 512], F32, tag="out_bank")
        nc.tensor.matmul(out=row_bank[:], lhsT=ones[:], rhs=row[:], start=True, stop=True)
        bias_bc = consts.tile([P, C], F32)
        nc.vector.tensor_copy(
            out=bias_bc[:].rearrange("p (e q) -> p e q", e=PARITIES),
            in_=row_bank[:, 0:C].rearrange("p (q e) -> p e q", e=PARITIES),
        )
        s_col = consts.tile([P, 1], F32)
        nc.vector.tensor_copy(out=s_col[:], in_=row_bank[:, S_AT : S_AT + 1])
        n_col = consts.tile([P, 1], F32)
        nc.vector.tensor_copy(out=n_col[:], in_=row_bank[:, N_AT : N_AT + 1])
        var_scale = consts.tile([P, 1], F32)
        nc.vector.tensor_scalar(
            out=var_scale[:], in0=s_col[:], scalar1=s_col[:, 0:1], scalar2=1.0 / C, op0=ALU.mult, op1=ALU.mult
        )
        gain = consts.tile([P, PARITIES], F32)
        nc.vector.tensor_scalar(
            out=gain[:], in0=ln_w[:], scalar1=n_col[:, 0:1], scalar2=s_col[:, 0:1], op0=ALU.mult, op1=ALU.mult
        )
        shift = consts.tile([P, PARITIES], F32)
        nc.vector.tensor_scalar(out=shift[:], in0=ln_b[:], scalar1=n_col[:, 0:1], scalar2=None, op0=ALU.mult)

        def transpose_in(grp, half):
            if half == 0:
                tiles["grouped", grp] = mx_pool.tile([P, TILES * K], BF16, name="h_grouped", align_bytes=64)
            h_words = tiles["h", grp][:].bitcast(F32)
            h_grouped_words = tiles["grouped", grp][:].bitcast(F32).rearrange(
                "p (t g c u) -> p t g c u", t=TILES, g=PASSES, u=2
            )
            for t in range(half * PAIR, (half + 1) * PAIR):
                h_bank = in_banks.tile([P, BLOCKS, P], F32, tag="in_bank")
                transpose_words(nc, h_bank, h_words[:, t * WORDS : (t + 1) * WORDS], ident)
                nc.scalar.copy(out=h_grouped_words[:, t, :, :, :], in_=words_by_column(h_bank))

        def quantise(grp, half):
            if half == 0:
                tiles["codes", grp] = mx_pool.tile([P, TILES * PASSES * P], U32, name="h_codes", align_bytes=64)
                tiles["scales", grp] = mx_pool.tile([P, TILES * PASSES * P], U8, name="h_scales", align_bytes=64)
            words = slice(half * PAIR * PASSES * P, (half + 1) * PAIR * PASSES * P)
            values = slice(half * PAIR * K, (half + 1) * PAIR * K)
            nc.vector.quantize_mx(
                out=tiles["codes", grp][:, words].bitcast(FP8X4),
                scales=tiles["scales", grp][:, words],
                in_=tiles["grouped", grp][:, values],
            )

        def multiply(grp, half):
            if half == 0:
                tiles["v", grp] = work.tile([P, TILES, C], F32, name="v")
                tiles["v_sum", grp] = stats.tile([P, TILES], F32, name="v_sum")
            h_codes = tiles["codes", grp]
            h_scales = tiles["scales", grp]
            acc = acc_banks.tile([P, PAIR, C], F32)
            for i in range(PAIR):
                for g in range(PASSES):
                    px = slice(((half * PAIR + i) * PASSES + g) * P, ((half * PAIR + i) * PASSES + g + 1) * P)
                    ch = slice(g * C, (g + 1) * C)
                    nc.tensor.matmul_mx(
                        out=acc[:, i, :],
                        lhsT=h_codes[:, px].bitcast(FP8X4),
                        lhsT_scale=h_scales[:, px],
                        rhs=w_codes[:, ch].bitcast(FP8X4),
                        rhs_scale=w_scales[:, ch],
                        start=(g == 0),
                        stop=(g == PASSES - 1),
                    )
            for i in range(PAIR):
                t = half * PAIR + i
                nc.vector.scalar_tensor_tensor(
                    out=tiles["v", grp][:, t, :],
                    in0=acc[:, i, :],
                    scalar=1.0,
                    in1=bias_bc[:],
                    op0=ALU.mult,
                    op1=ALU.add,
                    accum_out=tiles["v_sum", grp][:, t : t + 1],
                )

        def mean(grp):
            neg_mean = stats.tile([P, TILES], F32, name="neg_mean")
            nc.vector.tensor_scalar(
                out=neg_mean[:], in0=tiles["v_sum", grp][:], scalar1=-1.0 / C, scalar2=None, op0=ALU.mult
            )
            tiles["neg_mean", grp] = neg_mean

        def squares(grp):
            v = tiles["v", grp]
            neg_mean = tiles["neg_mean", grp]
            squared = work.tile([P, TILES, C], F32, name="squared")
            sq_sum = stats.tile([P, TILES], F32, name="sq_sum")
            for t in range(TILES):
                nc.scalar.activation(
                    out=squared[:, t, :],
                    in_=v[:, t, :],
                    func=ACT.Square,
                    bias=neg_mean[:, t : t + 1],
                    scale=1.0,
                    accum_out=sq_sum[:, t : t + 1],
                )
            std = stats.tile([P, TILES], F32, name="std")
            nc.scalar.activation(
                out=std[:], in_=sq_sum[:], func=ACT.Sqrt, bias=eps_col[:, 0:1], scale=var_scale[:, 0:1]
            )
            tiles["std", grp] = std

        def normalise(grp):
            v = tiles["v", grp]
            neg_mean = tiles["neg_mean", grp]
            rstd = stats.tile([P, TILES], F32, name="rstd")
            nc.vector.reciprocal(out=rstd[:], in_=tiles["std", grp][:])
            normed = work.tile([P, TILES, C], F32, name="normed")
            for t in range(TILES):
                nc.vector.tensor_scalar(
                    out=normed[:, t, :],
                    in0=v[:, t, :],
                    scalar1=neg_mean[:, t : t + 1],
                    scalar2=rstd[:, t : t + 1],
                    op0=ALU.add,
                    op1=ALU.mult,
                )
            tiles["normed", grp] = normed

        def transpose_out(grp, e):
            if e == 0:
                tiles["o", grp] = work.tile([P, IMAGES, PARITIES, IMAGE], F32, name="o_sb")
            o_bank = out_banks.tile([P, TILES, P], F32, tag="out_bank")
            for t in range(TILES):
                nc.tensor.transpose(o_bank[:, t, :], tiles["normed", grp][:, t, e * P : (e + 1) * P], ident[:])
            nc.vector.scalar_tensor_tensor(
                out=tiles["o", grp][:, :, e, :].rearrange("q b (p t) -> q b p t", t=TILES),
                in0=o_bank[:].rearrange("q t (b p) -> q b p t", b=IMAGES),
                scalar=gain[:, e : e + 1],
                in1=tiles["x", grp][:, :, e, :].rearrange("q b (p t) -> q b p t", t=TILES),
                op0=ALU.mult,
                op1=ALU.add,
            )

        def relu_store(grp):
            o_sb = tiles["o", grp]
            for e in range(PARITIES):
                nc.scalar.activation(
                    out=o_sb[:, :, e, :], in_=o_sb[:, :, e, :], func=ACT.Relu, bias=shift[:, e : e + 1], scale=1.0
                )
            nc.sync.dma_start(
                out=out[images_of(grp)].rearrange("b (q e) i j -> q b (e i j)", e=PARITIES),
                in_=o_sb[:].rearrange("q b e s -> q b (e s)"),
            )

        def is_group(grp):
            return 0 <= grp < GROUPS

        for step in range(GROUPS + 4):
            if is_group(step + PREFETCH):
                load(step + PREFETCH)

            if is_group(step):
                transpose_in(step, 0)
            if is_group(step - 1):
                multiply(step - 1, 0)
            if is_group(step - 4):
                transpose_out(step - 4, 1)
            if is_group(step):
                quantise(step, 0)
            if is_group(step - 2):
                squares(step - 2)

            if is_group(step):
                transpose_in(step, 1)
            if is_group(step - 1):
                multiply(step - 1, 1)
                mean(step - 1)
            if is_group(step - 3):
                transpose_out(step - 3, 0)
            if is_group(step - 2):
                normalise(step - 2)
            if is_group(step):
                quantise(step, 1)
            if is_group(step - 4):
                relu_store(step - 4)
